import numpy as np
import ml_dtypes


def mxq(x, axis, fmt="e4m3"):
    dtype, down = {"e4m3": (ml_dtypes.float8_e4m3fn, 7), "e5m2": (ml_dtypes.float8_e5m2, 14)}[fmt]
    v = np.moveaxis(np.asarray(x, np.float32).astype(ml_dtypes.bfloat16).astype(np.float64), axis, -1)
    blocks = v.reshape(v.shape[:-1] + (-1, 32))
    amax = np.abs(blocks).max(-1, keepdims=True)
    byte = np.maximum(np.where(amax > 0, np.frexp(amax)[1] - 1 + 127, 0) - down, 1)
    scale = np.exp2(byte - 127.0)
    codes = (blocks / scale).astype(np.float32).astype(dtype).astype(np.float64)
    return np.moveaxis((codes * scale).reshape(v.shape), -1, axis)


WIDE = False


def mx_kscale(k):
    if not WIDE:
        return np.ones(k)
    levels = np.array([10, -10, 5, -5, 0])
    a = np.random.permutation(np.resize(levels, k // 512 * 4)).reshape(k // 512, 4)
    idx = np.arange(k)
    return np.exp2(a[idx // 512, idx % 128 // 32])


BF16 = ml_dtypes.bfloat16


def bf(x):
    return np.asarray(x, np.float32).astype(BF16)


def f64(x):
    return np.asarray(x).astype(np.float64)


B, CH, CQ, CV, H, W = 1, 1024, 128, 512, 32, 64
EPS = 1e-5
POOL = 2
HW = H * W
HW4 = HW // (POOL * POOL)
A = 1.5 / CQ ** 0.25


def bn(y, s, b, m, v):
    inv = f64(s) / np.sqrt(f64(v) + EPS)
    return y * inv[None, :, None] + (f64(b) - f64(m) * inv)[None, :, None]


def maxpool(y):
    c = y.shape[1]
    return y.reshape(B, c, H // POOL, POOL, W // POOL, POOL).max(axis=(3, 5)).reshape(B, c, HW4)


def vec(c, z):
    return bf(z * np.random.standard_normal(c))


def pos(c):
    return bf(0.5 + np.random.random(c))


def setup_inputs():
    s = mx_kscale(CH)
    return {'memory': bf(np.random.standard_normal((B, CH, H, W)) * s[None, :, None, None]),
            'wq': bf(np.random.standard_normal((CQ, CH)) * A / np.sqrt(CH) / s), 'bq': vec(CQ, 0.1),
            'bnq_s': pos(CQ), 'bnq_b': vec(CQ, 0.1), 'bnq_m': vec(CQ, 0.1), 'bnq_v': pos(CQ),
            'wk': bf(np.random.standard_normal((CQ, CH)) * A / np.sqrt(CH) / s), 'bk': vec(CQ, 0.1),
            'bnk_s': pos(CQ), 'bnk_b': vec(CQ, 0.1), 'bnk_m': vec(CQ, 0.1), 'bnk_v': pos(CQ),
            'wv': bf(np.random.standard_normal((CV, CH)) / np.sqrt(CH) / s), 'bv': vec(CV, 0.3),
            'bnv_s': pos(CV), 'bnv_b': vec(CV, 0.3), 'bnv_m': vec(CV, 0.3), 'bnv_v': pos(CV)}


def reference(memory, wq, bq, bnq_s, bnq_b, bnq_m, bnq_v, wk, bk, bnk_s, bnk_b, bnk_m, bnk_v, wv, bv, bnv_s, bnv_b, bnv_m, bnv_v):
    mq = mxq(f64(memory).reshape(B, CH, HW), 1, 'e4m3')
    yq = (mxq(f64(wq), 1, 'e4m3') @ mq) + f64(bq)[None, :, None]
    yk = (mxq(f64(wk), 1, 'e4m3') @ mq) + f64(bk)[None, :, None]
    yv = (mxq(f64(wv), 1, 'e4m3') @ mq) + f64(bv)[None, :, None]
    q = bn(yq, bnq_s, bnq_b, bnq_m, bnq_v).transpose(0, 2, 1)
    k = maxpool(bn(yk, bnk_s, bnk_b, bnk_m, bnk_v))
    v = maxpool(bn(yv, bnv_s, bnv_b, bnv_m, bnv_v)).transpose(0, 2, 1)
    return q, k, v

@@ -1,0 +1,223 @@
+from contextlib import ExitStack
+
+import concourse.masks as masks
+import concourse.mybir as mybir
+
+F32 = mybir.dt.float32
+BF16 = mybir.dt.bfloat16
+U32 = mybir.dt.uint32
+U8 = mybir.dt.uint8
+FP8X4 = mybir.dt.float8_e4m3fn_x4
+IDENTITY = mybir.ActivationFunctionType.Identity
+
+P = 128
+PACK = 4
+K_PASS = P * PACK
+CH = 1024
+PASSES = CH // K_PASS
+WIDTH = 64
+POSITIONS = 32 * WIDTH
+CHUNK = 512
+CHUNKS = POSITIONS // CHUNK
+POOLED = CHUNK // 4
+BLOCKS = 6
+V_BLOCKS = 4
+POOL_BLOCKS = 1 + V_BLOCKS
+KINDS = 5
+EPS = 1e-5
+
+FLOPS = 2 * BLOCKS * P * CH * POSITIONS
+
+
+def tile_selfattention_pa_kernel(
+    tc,
+    memory,
+    wq, bq, bnq_s, bnq_b, bnq_m, bnq_v,
+    wk, bk, bnk_s, bnk_b, bnk_m, bnk_v,
+    wv, bv, bnv_s, bnv_b, bnv_m, bnv_v,
+    out_0, out_1, out_2,
+):
+    nc = tc.nc
+    with ExitStack() as ctx:
+        keep = ctx.enter_context(tc.tile_pool(name="keep", bufs=1))
+        resident = ctx.enter_context(tc.tile_pool(name="resident", bufs=CHUNKS))
+        stream = ctx.enter_context(tc.tile_pool(name="stream", bufs=2))
+        psum = ctx.enter_context(tc.psum_pool(name="psum", bufs=8))
+
+        identity = keep.tile([P, P], F32)
+        masks.make_identity(nc, identity[:])
+        warm = keep.tile([P, 1], F32)
+        nc.vector.memset(warm[:], 1.0)
+        nc.scalar.sqrt(out=warm[:], in_=warm[:])
+
+        vec_rows = keep.tile([P, P], BF16)
+        nc.vector.memset(vec_rows[:], 0.0)
+        q_vectors = (bq, bnq_s, bnq_b, bnq_m, bnq_v)
+        k_vectors = (bk, bnk_s, bnk_b, bnk_m, bnk_v)
+        v_vectors = (bv, bnv_s, bnv_b, bnv_m, bnv_v)
+
+        def load_vectors(queue, vectors, first_block, blocks):
+            for kind, vector in enumerate(vectors):
+                row = BLOCKS * kind + first_block
+                queue.dma_start(
+                    out=vec_rows[row : row + blocks, :],
+                    in_=vector.rearrange("(b c) -> b c", c=P),
+                )
+
+        mem_rows = memory.rearrange("b (j p e) h w -> p (b j) e (h w)", p=P, e=2)
+
+        def load_chunk(c):
+            raw = resident.tile([P, PASSES, PACK, CHUNK], BF16, name="mem_raw")
+            halves = raw[:].rearrange("p g (u e) n -> p (g u) e n", e=2)
+            for e in range(2):
+                nc.sync.dma_start(
+                    out=halves[:, :, e, :],
+                    in_=mem_rows[:, :, e, c * CHUNK : (c + 1) * CHUNK],
+                )
+            return raw
+
+        w_raw = keep.tile([P, BLOCKS, CH], BF16)
+        wv_blocks = wv.rearrange("(b r) k -> r b k", r=P)
+
+        load_vectors(nc.scalar, q_vectors, 0, 1)
+        load_vectors(nc.gpsimd, v_vectors, 2, V_BLOCKS)
+        mem_raw = [load_chunk(0)]
+        nc.sync.dma_start(out=w_raw[:, 0, :], in_=wq)
+        load_vectors(nc.scalar, k_vectors, 1, 1)
+        nc.sync.dma_start(out=w_raw[:, 1, :], in_=wk)
+        nc.sync.dma_start(out=w_raw[:, 2:4, :], in_=wv_blocks[:, 0:2, :])
+        nc.sync.dma_start(out=w_raw[:, 4:6, :], in_=wv_blocks[:, 2:4, :])
+        for c in range(1, CHUNKS):
+            mem_raw.append(load_chunk(c))
+
+        def quantise_chunk(c):
+            grouped = stream.tile([P, PASSES, CHUNK, PACK], BF16, align_bytes=64, name="grouped")
+            for g in range(PASSES):
+                nc.vector.tensor_copy(
+                    out=grouped[:, g, :, :].rearrange("p (c i) t -> p c t i", i=4),
+                    in_=mem_raw[c][:, g, :, :].rearrange("p t (c i) -> p c t i", i=4),
+                )
+            codes = stream.tile([P, PASSES, CHUNK], U32, align_bytes=64, name="codes")
+            scales = stream.tile([P, PASSES, CHUNK], U8, align_bytes=64, name="scales")
+            for g in range(PASSES):
+                nc.vector.quantize_mx(
+                    out=codes[:, g, :].bitcast(FP8X4),
+                    scales=scales[:, g, :],
+                    in_=grouped[:, g, :, :].rearrange("p n t -> p (n t)"),
+                )
+            return codes, scales
+
+        w_grouped = keep.tile([P, BLOCKS, CH], BF16, align_bytes=64)
+        w_codes = keep.tile([P, BLOCKS, PASSES * P], U32, align_bytes=64)
+        w_scales = keep.tile([P, BLOCKS, PASSES * P], U8, align_bytes=64)
+
+        def transpose_weights(m):
+            words = w_raw[:, m, :].bitcast(F32)
+            bank = psum.tile([P, CHUNK], F32, name="bank")
+            for j in range(PASSES * 2):
+                nc.tensor.transpose(bank[:, j * P : (j + 1) * P], words[:, j * P : (j + 1) * P], identity[:])
+            nc.scalar.copy(
+                out=w_grouped[:, m, :].bitcast(F32).rearrange("p (g r u) -> p g r u", g=PASSES, u=2),
+                in_=bank[:].rearrange("p (g u r) -> p g r u", g=PASSES, u=2),
+            )
+
+        def quantise_weights(first, blocks):
+            nc.vector.quantize_mx(
+                out=w_codes[:, first : first + blocks, :].rearrange("p m w -> p (m w)").bitcast(FP8X4),
+                scales=w_scales[:, first : first + blocks, :].rearrange("p m w -> p (m w)"),
+                in_=w_grouped[:, first : first + blocks, :].rearrange("p m k -> p (m k)"),
+            )
+
+        inv = keep.tile([P, BLOCKS], F32)
+        shift = keep.tile([P, BLOCKS], F32)
+
+        def fold_batch_norms():
+            vec_f32 = keep.tile([P, P], F32)
+            nc.vector.tensor_copy(out=vec_f32[:], in_=vec_rows[:])
+            bank = psum.tile([P, CHUNK], F32, name="bank")
+            nc.tensor.transpose(bank[:, 0:P], vec_f32[:], identity[:])
+            columns = keep.tile([P, KINDS, BLOCKS], F32)
+            nc.vector.tensor_copy(
+                out=columns[:].rearrange("p k b -> p (k b)"), in_=bank[:, 0 : KINDS * BLOCKS]
+            )
+            bias, gain, beta, mean, var = [columns[:, kind, :] for kind in range(KINDS)]
+            std = keep.tile([P, BLOCKS], F32)
+            nc.vector.tensor_scalar_add(out=std[:], in0=var, scalar1=EPS)
+            nc.scalar.sqrt(out=std[:], in_=std[:])
+            nc.vector.reciprocal(out=inv[:], in_=std[:])
+            nc.vector.tensor_mul(out=inv[:], in0=inv[:], in1=gain)
+            nc.vector.tensor_sub(out=shift[:], in0=bias, in1=mean)
+            nc.vector.tensor_mul(out=shift[:], in0=shift[:], in1=inv[:])
+            nc.vector.tensor_add(out=shift[:], in0=shift[:], in1=beta)
+
+        def project(m, codes, scales):
+            bank = psum.tile([P, CHUNK], F32, name="bank")
+            for g in range(PASSES):
+                nc.tensor.matmul_mx(
+                    out=bank[:],
+                    lhsT=w_codes[:, m, g * P : (g + 1) * P].bitcast(FP8X4),
+                    lhsT_scale=w_scales[:, m, g * P : (g + 1) * P],
+                    rhs=codes[:, g, :].bitcast(FP8X4),
+                    rhs_scale=scales[:, g, :],
+                    start=(g == 0),
+                    stop=(g == PASSES - 1),
+                )
+            return bank
+
+        def convolve_chunk(codes, scales):
+            zq = stream.tile([P, 4, P], F32, name="zq")
+            bank = project(0, codes, scales)
+            nc.scalar.activation(
+                out=zq[:], in_=bank[:].rearrange("p (j s) -> p s j", s=4),
+                func=IDENTITY, bias=shift[:, 0:1], scale=inv[:, 0:1],
+            )
+            z = stream.tile([P, POOL_BLOCKS, CHUNK], F32, name="z")
+            for b in range(POOL_BLOCKS):
+                m = 1 + b
+                bank = project(m, codes, scales)
+                nc.scalar.activation(
+                    out=z[:, b, :], in_=bank[:],
+                    func=IDENTITY, bias=shift[:, m : m + 1], scale=inv[:, m : m + 1],
+                )
+            return zq, z
+
+        pooled = keep.tile([P, POOL_BLOCKS, CHUNKS, POOLED], F32)
+
+        def finish_chunk(c, zq, z):
+            row_pairs = z[:].rearrange("p b (a d w) -> p (b a) d w", d=2, w=WIDTH)
+            row_max = stream.tile([P, POOL_BLOCKS * CHUNK // (2 * WIDTH), WIDTH], F32, name="row_max")
+            nc.vector.tensor_max(out=row_max[:], in0=row_pairs[:, :, 0, :], in1=row_pairs[:, :, 1, :])
+            column_pairs = row_max[:].rearrange("p (b a) (x d) -> p b (a x) d", b=POOL_BLOCKS, d=2)
+            nc.vector.tensor_max(
+                out=pooled[:, :, c, :], in0=column_pairs[:, :, :, 0], in1=column_pairs[:, :, :, 1]
+            )
+
+            q_bank = psum.tile([P, CHUNK], F32, name="bank")
+            for s in range(4):
+                nc.tensor.transpose(q_bank[:, s * P : (s + 1) * P], zq[:, s, :], identity[:])
+            v_bank = psum.tile([P, CHUNK], F32, name="bank")
+            for b in range(V_BLOCKS):
+                nc.tensor.transpose(v_bank[:, b * P : (b + 1) * P], pooled[:, 1 + b, c, :], identity[:])
+            q_rows = stream.tile([P, CHUNK], F32, name="q_rows")
+            nc.scalar.copy(out=q_rows[:], in_=q_bank[:])
+            nc.sync.dma_start(
+                out=out_0[0, c * CHUNK : (c + 1) * CHUNK, :].rearrange("(j s) ch -> j (s ch)", s=4),
+                in_=q_rows[:],
+            )
+            v_rows = stream.tile([P, CHUNK], F32, name="v_rows")
+            nc.scalar.copy(out=v_rows[:], in_=v_bank[:])
+            nc.sync.dma_start(out=out_2[0, c * POOLED : (c + 1) * POOLED, :], in_=v_rows[:])
+
+        quantised = [quantise_chunk(0)]
+        for first in range(0, BLOCKS, 2):
+            transpose_weights(first)
+            transpose_weights(first + 1)
+            quantise_weights(first, 2)
+        fold_batch_norms()
+        results = [convolve_chunk(*quantised[0])]
+        for c in range(1, CHUNKS):
+            quantised.append(quantise_chunk(c))
+            results.append(convolve_chunk(*quantised[c]))
+            finish_chunk(c - 1, *results[c - 1])
+        finish_chunk(CHUNKS - 1, *results[CHUNKS - 1])
+        nc.sync.dma_start(out=out_1[0], in_=pooled[:, 0, :, :].rearrange("p c x -> p (c x)"))

@@ -43,12 +43,10 @@ def tile_selfattention_pa_kernel(
         resident = ctx.enter_context(tc.tile_pool(name="resident", bufs=CHUNKS))
         stream = ctx.enter_context(tc.tile_pool(name="stream", bufs=2))
         psum = ctx.enter_context(tc.psum_pool(name="psum", bufs=8))
+        ctx.enter_context(tc.manual_schedule())
 
         identity = keep.tile([P, P], F32)
         masks.make_identity(nc, identity[:])
-        warm = keep.tile([P, 1], F32)
-        nc.vector.memset(warm[:], 1.0)
-        nc.scalar.sqrt(out=warm[:], in_=warm[:])
 
         vec_rows = keep.tile([P, P], BF16)
         nc.vector.memset(vec_rows[:], 0.0)
@@ -90,10 +88,15 @@ def tile_selfattention_pa_kernel(
         for c in range(1, CHUNKS):
             mem_raw.append(load_chunk(c))
 
+        warm = keep.tile([P, 1], F32)
+        nc.vector.memset(warm[:], 1.0)
+        nc.scalar.sqrt(out=warm[:], in_=warm[:])
+
         def quantise_chunk(c):
             grouped = stream.tile([P, PASSES, CHUNK, PACK], BF16, align_bytes=64, name="grouped")
             for g in range(PASSES):
-                nc.vector.tensor_copy(
+                copy = nc.scalar.copy if (c == 0 and g == 1) else nc.vector.tensor_copy
+                copy(
                     out=grouped[:, g, :, :].rearrange("p (c i) t -> p c t i", i=4),
                     in_=mem_raw[c][:, g, :, :].rearrange("p t (c i) -> p c t i", i=4),
                 )
@@ -131,22 +134,25 @@ def tile_selfattention_pa_kernel(
         inv = keep.tile([P, BLOCKS], F32)
         shift = keep.tile([P, BLOCKS], F32)
 
-        def fold_batch_norms():
+        columns = keep.tile([P, KINDS, BLOCKS], F32)
+        bias, gain, beta, mean, var = [columns[:, kind, :] for kind in range(KINDS)]
+        std = keep.tile([P, BLOCKS], F32)
+
+        def turn_vectors():
             vec_f32 = keep.tile([P, P], F32)
             nc.vector.tensor_copy(out=vec_f32[:], in_=vec_rows[:])
             bank = psum.tile([P, CHUNK], F32, name="bank")
             nc.tensor.transpose(bank[:, 0:P], vec_f32[:], identity[:])
-            columns = keep.tile([P, KINDS, BLOCKS], F32)
             nc.vector.tensor_copy(
                 out=columns[:].rearrange("p k b -> p (k b)"), in_=bank[:, 0 : KINDS * BLOCKS]
             )
-            bias, gain, beta, mean, var = [columns[:, kind, :] for kind in range(KINDS)]
-            std = keep.tile([P, BLOCKS], F32)
             nc.vector.tensor_scalar_add(out=std[:], in0=var, scalar1=EPS)
             nc.scalar.sqrt(out=std[:], in_=std[:])
+            nc.vector.tensor_sub(out=shift[:], in0=bias, in1=mean)
+
+        def fold_batch_norms():
             nc.vector.reciprocal(out=inv[:], in_=std[:])
             nc.vector.tensor_mul(out=inv[:], in0=inv[:], in1=gain)
-            nc.vector.tensor_sub(out=shift[:], in0=bias, in1=mean)
             nc.vector.tensor_mul(out=shift[:], in0=shift[:], in1=inv[:])
             nc.vector.tensor_add(out=shift[:], in0=shift[:], in1=beta)
 
@@ -171,7 +177,7 @@ def tile_selfattention_pa_kernel(
                 out=zq[:], in_=bank[:].rearrange("p (j s) -> p s j", s=4),
                 func=IDENTITY, bias=shift[:, 0:1], scale=inv[:, 0:1],
             )
-            z = stream.tile([P, POOL_BLOCKS, CHUNK], F32, name="z")
+            z = stream.tile([P, POOL_BLOCKS, CHUNK], F32, name="z", bufs=3)
             for b in range(POOL_BLOCKS):
                 m = 1 + b
                 bank = project(m, codes, scales)
@@ -183,7 +189,18 @@ def tile_selfattention_pa_kernel(
 
         pooled = keep.tile([P, POOL_BLOCKS, CHUNKS, POOLED], F32)
 
-        def finish_chunk(c, zq, z):
+        def finish_q(c, zq):
+            q_bank = psum.tile([P, CHUNK], F32, name="bank")
+            for s in range(4):
+                nc.tensor.transpose(q_bank[:, s * P : (s + 1) * P], zq[:, s, :], identity[:])
+            q_rows = stream.tile([P, CHUNK], F32, name="q_rows")
+            nc.scalar.copy(out=q_rows[:], in_=q_bank[:])
+            nc.sync.dma_start(
+                out=out_0[0, c * CHUNK : (c + 1) * CHUNK, :].rearrange("(j s) ch -> j (s ch)", s=4),
+                in_=q_rows[:],
+            )
+
+        def finish_kv(c, z):
             row_pairs = z[:].rearrange("p b (a d w) -> p (b a) d w", d=2, w=WIDTH)
             row_max = stream.tile([P, POOL_BLOCKS * CHUNK // (2 * WIDTH), WIDTH], F32, name="row_max")
             nc.vector.tensor_max(out=row_max[:], in0=row_pairs[:, :, 0, :], in1=row_pairs[:, :, 1, :])
@@ -192,32 +209,32 @@ def tile_selfattention_pa_kernel(
                 out=pooled[:, :, c, :], in0=column_pairs[:, :, :, 0], in1=column_pairs[:, :, :, 1]
             )
 
-            q_bank = psum.tile([P, CHUNK], F32, name="bank")
-            for s in range(4):
-                nc.tensor.transpose(q_bank[:, s * P : (s + 1) * P], zq[:, s, :], identity[:])
             v_bank = psum.tile([P, CHUNK], F32, name="bank")
             for b in range(V_BLOCKS):
                 nc.tensor.transpose(v_bank[:, b * P : (b + 1) * P], pooled[:, 1 + b, c, :], identity[:])
-            q_rows = stream.tile([P, CHUNK], F32, name="q_rows")
-            nc.scalar.copy(out=q_rows[:], in_=q_bank[:])
-            nc.sync.dma_start(
-                out=out_0[0, c * CHUNK : (c + 1) * CHUNK, :].rearrange("(j s) ch -> j (s ch)", s=4),
-                in_=q_rows[:],
-            )
             v_rows = stream.tile([P, CHUNK], F32, name="v_rows")
             nc.scalar.copy(out=v_rows[:], in_=v_bank[:])
             nc.sync.dma_start(out=out_2[0, c * POOLED : (c + 1) * POOLED, :], in_=v_rows[:])
 
         quantised = [quantise_chunk(0)]
-        for first in range(0, BLOCKS, 2):
-            transpose_weights(first)
-            transpose_weights(first + 1)
-            quantise_weights(first, 2)
+        transpose_weights(0)
+        transpose_weights(1)
+        quantise_weights(0, 2)
+        transpose_weights(2)
+        transpose_weights(3)
+        turn_vectors()
+        quantise_weights(2, 2)
         fold_batch_norms()
-        results = [convolve_chunk(*quantised[0])]
-        for c in range(1, CHUNKS):
-            quantised.append(quantise_chunk(c))
-            results.append(convolve_chunk(*quantised[c]))
-            finish_chunk(c - 1, *results[c - 1])
-        finish_chunk(CHUNKS - 1, *results[CHUNKS - 1])
+        transpose_weights(4)
+        transpose_weights(5)
+        quantise_weights(4, 2)
+        results = []
+        for c in range(CHUNKS + 2):
+            if c < CHUNKS:
+                if c > 0:
+                    quantised.append(quantise_chunk(c))
+                results.append(convolve_chunk(*quantised[c]))
+                finish_q(c, results[c][0])
+            if c >= 2:
+                finish_kv(c - 2, results[c - 2][1])
         nc.sync.dma_start(out=out_1[0], in_=pooled[:, 0, :, :].rearrange("p c x -> p (c x)"))

@@ -46,7 +46,8 @@ def tile_selfattention_pa_kernel(
         ctx.enter_context(tc.manual_schedule())
 
         identity = keep.tile([P, P], F32)
-        masks.make_identity(nc, identity[:])
+        nc.vector.memset(identity[:], 0.0)
+        masks.make_identity(nc, identity[:], nomemset=True)
 
         vec_rows = keep.tile([P, P], BF16)
         nc.vector.memset(vec_rows[:], 0.0)
@@ -208,6 +209,7 @@ def tile_selfattention_pa_kernel(
             nc.vector.tensor_max(
                 out=pooled[:, :, c, :], in0=column_pairs[:, :, :, 0], in1=column_pairs[:, :, :, 1]
             )
+            nc.sync.dma_start(out=out_1[0, :, c * POOLED : (c + 1) * POOLED], in_=pooled[:, 0, c, :])
 
             v_bank = psum.tile([P, CHUNK], F32, name="bank")
             for b in range(V_BLOCKS):
@@ -222,11 +224,11 @@ def tile_selfattention_pa_kernel(
         quantise_weights(0, 2)
         transpose_weights(2)
         transpose_weights(3)
-        turn_vectors()
         quantise_weights(2, 2)
-        fold_batch_norms()
         transpose_weights(4)
         transpose_weights(5)
+        turn_vectors()
+        fold_batch_norms()
         quantise_weights(4, 2)
         results = []
         for c in range(CHUNKS + 2):
@@ -237,4 +239,3 @@ def tile_selfattention_pa_kernel(
                 finish_q(c, results[c][0])
             if c >= 2:
                 finish_kv(c - 2, results[c - 2][1])
-        nc.sync.dma_start(out=out_1[0], in_=pooled[:, 0, :, :].rearrange("p c x -> p (c x)"))

@@ -20,9 +20,11 @@ POSITIONS = 32 * WIDTH
 CHUNK = 512
 CHUNKS = POSITIONS // CHUNK
 POOLED = CHUNK // 4
-BLOCKS = 6
 V_BLOCKS = 4
-POOL_BLOCKS = 1 + V_BLOCKS
+Q_BLOCK = 4
+K_BLOCK = 5
+BLOCKS = 6
+POOL_BLOCKS = V_BLOCKS + 1
 KINDS = 5
 EPS = 1e-5
 
@@ -45,20 +47,23 @@ def tile_selfattention_pa_kernel(
         psum = ctx.enter_context(tc.psum_pool(name="psum", bufs=8))
         ctx.enter_context(tc.manual_schedule())
 
+
+        vec_rows = keep.tile([P, P], BF16)
+        nc.gpsimd.memset(vec_rows[:], 0.0)
         identity = keep.tile([P, P], F32)
         nc.vector.memset(identity[:], 0.0)
         masks.make_identity(nc, identity[:], nomemset=True)
-
-        vec_rows = keep.tile([P, P], BF16)
-        nc.vector.memset(vec_rows[:], 0.0)
+        warm = keep.tile([P, 1], F32)
+        nc.vector.memset(warm[:], 1.0)
+        nc.scalar.sqrt(out=warm[:], in_=warm[:])
         q_vectors = (bq, bnq_s, bnq_b, bnq_m, bnq_v)
         k_vectors = (bk, bnk_s, bnk_b, bnk_m, bnk_v)
         v_vectors = (bv, bnv_s, bnv_b, bnv_m, bnv_v)
 
-        def load_vectors(queue, vectors, first_block, blocks):
+        def load_vectors(vectors, first_block, blocks):
             for kind, vector in enumerate(vectors):
                 row = BLOCKS * kind + first_block
-                queue.dma_start(
+                nc.sync.dma_start(
                     out=vec_rows[row : row + blocks, :],
                     in_=vector.rearrange("(b c) -> b c", c=P),
                 )
@@ -78,26 +83,21 @@ def tile_selfattention_pa_kernel(
         w_raw = keep.tile([P, BLOCKS, CH], BF16)
         wv_blocks = wv.rearrange("(b r) k -> r b k", r=P)
 
-        load_vectors(nc.scalar, q_vectors, 0, 1)
-        load_vectors(nc.gpsimd, v_vectors, 2, V_BLOCKS)
+        load_vectors(v_vectors, 0, V_BLOCKS)
         mem_raw = [load_chunk(0)]
-        nc.sync.dma_start(out=w_raw[:, 0, :], in_=wq)
-        load_vectors(nc.scalar, k_vectors, 1, 1)
-        nc.sync.dma_start(out=w_raw[:, 1, :], in_=wk)
-        nc.sync.dma_start(out=w_raw[:, 2:4, :], in_=wv_blocks[:, 0:2, :])
-        nc.sync.dma_start(out=w_raw[:, 4:6, :], in_=wv_blocks[:, 2:4, :])
+        nc.sync.dma_start(out=w_raw[:, 0:2, :], in_=wv_blocks[:, 0:2, :])
+        load_vectors(q_vectors, Q_BLOCK, 1)
+        nc.sync.dma_start(out=w_raw[:, 2:4, :], in_=wv_blocks[:, 2:4, :])
+        nc.sync.dma_start(out=w_raw[:, Q_BLOCK, :], in_=wq)
+        nc.sync.dma_start(out=w_raw[:, K_BLOCK, :], in_=wk)
+        load_vectors(k_vectors, K_BLOCK, 1)
         for c in range(1, CHUNKS):
             mem_raw.append(load_chunk(c))
-
-        warm = keep.tile([P, 1], F32)
-        nc.vector.memset(warm[:], 1.0)
-        nc.scalar.sqrt(out=warm[:], in_=warm[:])
 
         def quantise_chunk(c):
             grouped = stream.tile([P, PASSES, CHUNK, PACK], BF16, align_bytes=64, name="grouped")
             for g in range(PASSES):
-                copy = nc.scalar.copy if (c == 0 and g == 1) else nc.vector.tensor_copy
-                copy(
+                nc.vector.tensor_copy(
                     out=grouped[:, g, :, :].rearrange("p (c i) t -> p c t i", i=4),
                     in_=mem_raw[c][:, g, :, :].rearrange("p t (c i) -> p c t i", i=4),
                 )
@@ -139,9 +139,12 @@ def tile_selfattention_pa_kernel(
         bias, gain, beta, mean, var = [columns[:, kind, :] for kind in range(KINDS)]
         std = keep.tile([P, BLOCKS], F32)
 
-        def turn_vectors():
-            vec_f32 = keep.tile([P, P], F32)
+        vec_f32 = keep.tile([P, P], F32)
+
+        def widen_vectors():
             nc.vector.tensor_copy(out=vec_f32[:], in_=vec_rows[:])
+
+        def turn_vectors():
             bank = psum.tile([P, CHUNK], F32, name="bank")
             nc.tensor.transpose(bank[:, 0:P], vec_f32[:], identity[:])
             nc.vector.tensor_copy(
@@ -172,29 +175,26 @@ def tile_selfattention_pa_kernel(
             return bank
 
         def convolve_chunk(codes, scales):
-            zq = stream.tile([P, 4, P], F32, name="zq")
-            bank = project(0, codes, scales)
-            nc.scalar.activation(
-                out=zq[:], in_=bank[:].rearrange("p (j s) -> p s j", s=4),
-                func=IDENTITY, bias=shift[:, 0:1], scale=inv[:, 0:1],
-            )
             z = stream.tile([P, POOL_BLOCKS, CHUNK], F32, name="z", bufs=3)
-            for b in range(POOL_BLOCKS):
-                m = 1 + b
+            zq = stream.tile([P, 4, P], F32, name="zq")
+            for m in range(BLOCKS):
                 bank = project(m, codes, scales)
+                if m == Q_BLOCK:
+                    source, target = bank[:].rearrange("p (j s) -> p s j", s=4), zq[:]
+                else:
+                    source, target = bank[:], z[:, min(m, V_BLOCKS), :]
                 nc.scalar.activation(
-                    out=z[:, b, :], in_=bank[:],
+                    out=target, in_=source,
                     func=IDENTITY, bias=shift[:, m : m + 1], scale=inv[:, m : m + 1],
                 )
             return zq, z
 
-        pooled = keep.tile([P, POOL_BLOCKS, CHUNKS, POOLED], F32)
 
         def finish_q(c, zq):
             q_bank = psum.tile([P, CHUNK], F32, name="bank")
             for s in range(4):
                 nc.tensor.transpose(q_bank[:, s * P : (s + 1) * P], zq[:, s, :], identity[:])
-            q_rows = stream.tile([P, CHUNK], F32, name="q_rows")
+            q_rows = resident.tile([P, CHUNK], F32, name="q_rows")
             nc.scalar.copy(out=q_rows[:], in_=q_bank[:])
             nc.sync.dma_start(
                 out=out_0[0, c * CHUNK : (c + 1) * CHUNK, :].rearrange("(j s) ch -> j (s ch)", s=4),
@@ -206,15 +206,18 @@ def tile_selfattention_pa_kernel(
             row_max = stream.tile([P, POOL_BLOCKS * CHUNK // (2 * WIDTH), WIDTH], F32, name="row_max")
             nc.vector.tensor_max(out=row_max[:], in0=row_pairs[:, :, 0, :], in1=row_pairs[:, :, 1, :])
             column_pairs = row_max[:].rearrange("p (b a) (x d) -> p b (a x) d", b=POOL_BLOCKS, d=2)
+            pooled = stream.tile([P, POOL_BLOCKS, POOLED], F32, name="pooled", bufs=3)
             nc.vector.tensor_max(
-                out=pooled[:, :, c, :], in0=column_pairs[:, :, :, 0], in1=column_pairs[:, :, :, 1]
+                out=pooled[:], in0=column_pairs[:, :, :, 0], in1=column_pairs[:, :, :, 1]
             )
-            nc.sync.dma_start(out=out_1[0, :, c * POOLED : (c + 1) * POOLED], in_=pooled[:, 0, c, :])
+            nc.sync.dma_start(
+                out=out_1[0, :, c * POOLED : (c + 1) * POOLED], in_=pooled[:, V_BLOCKS, :]
+            )
 
             v_bank = psum.tile([P, CHUNK], F32, name="bank")
             for b in range(V_BLOCKS):
-                nc.tensor.transpose(v_bank[:, b * P : (b + 1) * P], pooled[:, 1 + b, c, :], identity[:])
-            v_rows = stream.tile([P, CHUNK], F32, name="v_rows")
+                nc.tensor.transpose(v_bank[:, b * P : (b + 1) * P], pooled[:, b, :], identity[:])
+            v_rows = resident.tile([P, CHUNK], F32, name="v_rows")
             nc.scalar.copy(out=v_rows[:], in_=v_bank[:])
             nc.sync.dma_start(out=out_2[0, c * POOLED : (c + 1) * POOLED, :], in_=v_rows[:])
 
@@ -222,14 +225,15 @@ def tile_selfattention_pa_kernel(
         transpose_weights(0)
         transpose_weights(1)
         quantise_weights(0, 2)
+        widen_vectors()
         transpose_weights(2)
         transpose_weights(3)
-        quantise_weights(2, 2)
-        transpose_weights(4)
-        transpose_weights(5)
+        transpose_weights(Q_BLOCK)
         turn_vectors()
+        quantise_weights(2, 2)
+        transpose_weights(K_BLOCK)
         fold_batch_norms()
-        quantise_weights(4, 2)
+        quantise_weights(Q_BLOCK, 2)
         results = []
         for c in range(CHUNKS + 2):
             if c < CHUNKS:

@@ -21,8 +21,8 @@ CHUNK = 512
 CHUNKS = POSITIONS // CHUNK
 POOLED = CHUNK // 4
 V_BLOCKS = 4
-Q_BLOCK = 4
-K_BLOCK = 5
+K_BLOCK = 4
+Q_BLOCK = 5
 BLOCKS = 6
 POOL_BLOCKS = V_BLOCKS + 1
 KINDS = 5
@@ -86,11 +86,11 @@ def tile_selfattention_pa_kernel(
         load_vectors(v_vectors, 0, V_BLOCKS)
         mem_raw = [load_chunk(0)]
         nc.sync.dma_start(out=w_raw[:, 0:2, :], in_=wv_blocks[:, 0:2, :])
-        load_vectors(q_vectors, Q_BLOCK, 1)
-        nc.sync.dma_start(out=w_raw[:, 2:4, :], in_=wv_blocks[:, 2:4, :])
-        nc.sync.dma_start(out=w_raw[:, Q_BLOCK, :], in_=wq)
-        nc.sync.dma_start(out=w_raw[:, K_BLOCK, :], in_=wk)
         load_vectors(k_vectors, K_BLOCK, 1)
+        nc.sync.dma_start(out=w_raw[:, 2:4, :], in_=wv_blocks[:, 2:4, :])
+        nc.sync.dma_start(out=w_raw[:, K_BLOCK, :], in_=wk)
+        nc.sync.dma_start(out=w_raw[:, Q_BLOCK, :], in_=wq)
+        load_vectors(q_vectors, Q_BLOCK, 1)
         for c in range(1, CHUNKS):
             mem_raw.append(load_chunk(c))
 
@@ -228,12 +228,12 @@ def tile_selfattention_pa_kernel(
         widen_vectors()
         transpose_weights(2)
         transpose_weights(3)
-        transpose_weights(Q_BLOCK)
+        transpose_weights(K_BLOCK)
         turn_vectors()
         quantise_weights(2, 2)
-        transpose_weights(K_BLOCK)
+        transpose_weights(Q_BLOCK)
         fold_batch_norms()
-        quantise_weights(Q_BLOCK, 2)
+        quantise_weights(K_BLOCK, 2)
         results = []
         for c in range(CHUNKS + 2):
             if c < CHUNKS:

from contextlib import ExitStack

import concourse.masks as masks
import concourse.mybir as mybir

F32 = mybir.dt.float32
BF16 = mybir.dt.bfloat16
U32 = mybir.dt.uint32
U8 = mybir.dt.uint8
FP8X4 = mybir.dt.float8_e4m3fn_x4
IDENTITY = mybir.ActivationFunctionType.Identity

P = 128
PACK = 4
K_PASS = P * PACK
CH = 1024
PASSES = CH // K_PASS
WIDTH = 64
POSITIONS = 32 * WIDTH
CHUNK = 512
CHUNKS = POSITIONS // CHUNK
POOLED = CHUNK // 4
V_BLOCKS = 4
K_BLOCK = 4
Q_BLOCK = 5
BLOCKS = 6
POOL_BLOCKS = V_BLOCKS + 1
KINDS = 5
EPS = 1e-5

FLOPS = 2 * BLOCKS * P * CH * POSITIONS


def tile_selfattention_pa_kernel(
    tc,
    memory,
    wq, bq, bnq_s, bnq_b, bnq_m, bnq_v,
    wk, bk, bnk_s, bnk_b, bnk_m, bnk_v,
    wv, bv, bnv_s, bnv_b, bnv_m, bnv_v,
    out_0, out_1, out_2,
):
    nc = tc.nc
    with ExitStack() as ctx:
        keep = ctx.enter_context(tc.tile_pool(name="keep", bufs=1))
        resident = ctx.enter_context(tc.tile_pool(name="resident", bufs=CHUNKS))
        stream = ctx.enter_context(tc.tile_pool(name="stream", bufs=2))
        psum = ctx.enter_context(tc.psum_pool(name="psum", bufs=8))
        ctx.enter_context(tc.manual_schedule())


        vec_rows = keep.tile([P, P], BF16)
        nc.gpsimd.memset(vec_rows[:], 0.0)
        identity = keep.tile([P, P], F32)
        nc.vector.memset(identity[:], 0.0)
        masks.make_identity(nc, identity[:], nomemset=True)
        warm = keep.tile([P, 1], F32)
        nc.vector.memset(warm[:], 1.0)
        nc.scalar.sqrt(out=warm[:], in_=warm[:])
        q_vectors = (bq, bnq_s, bnq_b, bnq_m, bnq_v)
        k_vectors = (bk, bnk_s, bnk_b, bnk_m, bnk_v)
        v_vectors = (bv, bnv_s, bnv_b, bnv_m, bnv_v)

        def load_vectors(vectors, first_block, blocks):
            for kind, vector in enumerate(vectors):
                row = BLOCKS * kind + first_block
                nc.sync.dma_start(
                    out=vec_rows[row : row + blocks, :],
                    in_=vector.rearrange("(b c) -> b c", c=P),
                )

        mem_rows = memory.rearrange("b (j p e) h w -> p (b j) e (h w)", p=P, e=2)

        def load_chunk(c):
            raw = resident.tile([P, PASSES, PACK, CHUNK], BF16, name="mem_raw")
            halves = raw[:].rearrange("p g (u e) n -> p (g u) e n", e=2)
            for e in range(2):
                nc.sync.dma_start(
                    out=halves[:, :, e, :],
                    in_=mem_rows[:, :, e, c * CHUNK : (c + 1) * CHUNK],
                )
            return raw

        w_raw = keep.tile([P, BLOCKS, CH], BF16)
        wv_blocks = wv.rearrange("(b r) k -> r b k", r=P)

        load_vectors(v_vectors, 0, V_BLOCKS)
        mem_raw = [load_chunk(0)]
        nc.sync.dma_start(out=w_raw[:, 0:2, :], in_=wv_blocks[:, 0:2, :])
        load_vectors(k_vectors, K_BLOCK, 1)
        nc.sync.dma_start(out=w_raw[:, 2:4, :], in_=wv_blocks[:, 2:4, :])
        nc.sync.dma_start(out=w_raw[:, K_BLOCK, :], in_=wk)
        nc.sync.dma_start(out=w_raw[:, Q_BLOCK, :], in_=wq)
        load_vectors(q_vectors, Q_BLOCK, 1)
        for c in range(1, CHUNKS):
            mem_raw.append(load_chunk(c))

        def quantise_chunk(c):
            grouped = stream.tile([P, PASSES, CHUNK, PACK], BF16, align_bytes=64, name="grouped")
            for g in range(PASSES):
                nc.vector.tensor_copy(
                    out=grouped[:, g, :, :].rearrange("p (c i) t -> p c t i", i=4),
                    in_=mem_raw[c][:, g, :, :].rearrange("p t (c i) -> p c t i", i=4),
                )
            codes = stream.tile([P, PASSES, CHUNK], U32, align_bytes=64, name="codes")
            scales = stream.tile([P, PASSES, CHUNK], U8, align_bytes=64, name="scales")
            for g in range(PASSES):
                nc.vector.quantize_mx(
                    out=codes[:, g, :].bitcast(FP8X4),
                    scales=scales[:, g, :],
                    in_=grouped[:, g, :, :].rearrange("p n t -> p (n t)"),
                )
            return codes, scales

        w_grouped = keep.tile([P, BLOCKS, CH], BF16, align_bytes=64)
        w_codes = keep.tile([P, BLOCKS, PASSES * P], U32, align_bytes=64)
        w_scales = keep.tile([P, BLOCKS, PASSES * P], U8, align_bytes=64)

        def transpose_weights(m):
            words = w_raw[:, m, :].bitcast(F32)
            bank = psum.tile([P, CHUNK], F32, name="bank")
            for j in range(PASSES * 2):
                nc.tensor.transpose(bank[:, j * P : (j + 1) * P], words[:, j * P : (j + 1) * P], identity[:])
            nc.scalar.copy(
                out=w_grouped[:, m, :].bitcast(F32).rearrange("p (g r u) -> p g r u", g=PASSES, u=2),
                in_=bank[:].rearrange("p (g u r) -> p g r u", g=PASSES, u=2),
            )

        def quantise_weights(first, blocks):
            nc.vector.quantize_mx(
                out=w_codes[:, first : first + blocks, :].rearrange("p m w -> p (m w)").bitcast(FP8X4),
                scales=w_scales[:, first : first + blocks, :].rearrange("p m w -> p (m w)"),
                in_=w_grouped[:, first : first + blocks, :].rearrange("p m k -> p (m k)"),
            )

        inv = keep.tile([P, BLOCKS], F32)
        shift = keep.tile([P, BLOCKS], F32)

        columns = keep.tile([P, KINDS, BLOCKS], F32)
        bias, gain, beta, mean, var = [columns[:, kind, :] for kind in range(KINDS)]
        std = keep.tile([P, BLOCKS], F32)

        vec_f32 = keep.tile([P, P], F32)

        def widen_vectors():
            nc.vector.tensor_copy(out=vec_f32[:], in_=vec_rows[:])

        def turn_vectors():
            bank = psum.tile([P, CHUNK], F32, name="bank")
            nc.tensor.transpose(bank[:, 0:P], vec_f32[:], identity[:])
            nc.vector.tensor_copy(
                out=columns[:].rearrange("p k b -> p (k b)"), in_=bank[:, 0 : KINDS * BLOCKS]
            )
            nc.vector.tensor_scalar_add(out=std[:], in0=var, scalar1=EPS)
            nc.scalar.sqrt(out=std[:], in_=std[:])
            nc.vector.tensor_sub(out=shift[:], in0=bias, in1=mean)

        def fold_batch_norms():
            nc.vector.reciprocal(out=inv[:], in_=std[:])
            nc.vector.tensor_mul(out=inv[:], in0=inv[:], in1=gain)
            nc.vector.tensor_mul(out=shift[:], in0=shift[:], in1=inv[:])
            nc.vector.tensor_add(out=shift[:], in0=shift[:], in1=beta)

        def project(m, codes, scales):
            bank = psum.tile([P, CHUNK], F32, name="bank")
            for g in range(PASSES):
                nc.tensor.matmul_mx(
                    out=bank[:],
                    lhsT=w_codes[:, m, g * P : (g + 1) * P].bitcast(FP8X4),
                    lhsT_scale=w_scales[:, m, g * P : (g + 1) * P],
                    rhs=codes[:, g, :].bitcast(FP8X4),
                    rhs_scale=scales[:, g, :],
                    start=(g == 0),
                    stop=(g == PASSES - 1),
                )
            return bank

        def convolve_chunk(codes, scales):
            z = stream.tile([P, POOL_BLOCKS, CHUNK], F32, name="z", bufs=3)
            zq = stream.tile([P, 4, P], F32, name="zq")
            for m in range(BLOCKS):
                bank = project(m, codes, scales)
                if m == Q_BLOCK:
                    source, target = bank[:].rearrange("p (j s) -> p s j", s=4), zq[:]
                else:
                    source, target = bank[:], z[:, min(m, V_BLOCKS), :]
                nc.scalar.activation(
                    out=target, in_=source,
                    func=IDENTITY, bias=shift[:, m : m + 1], scale=inv[:, m : m + 1],
                )
            return zq, z


        def finish_q(c, zq):
            q_bank = psum.tile([P, CHUNK], F32, name="bank")
            for s in range(4):
                nc.tensor.transpose(q_bank[:, s * P : (s + 1) * P], zq[:, s, :], identity[:])
            q_rows = resident.tile([P, CHUNK], F32, name="q_rows")
            nc.scalar.copy(out=q_rows[:], in_=q_bank[:])
            nc.sync.dma_start(
                out=out_0[0, c * CHUNK : (c + 1) * CHUNK, :].rearrange("(j s) ch -> j (s ch)", s=4),
                in_=q_rows[:],
            )

        def finish_kv(c, z):
            row_pairs = z[:].rearrange("p b (a d w) -> p (b a) d w", d=2, w=WIDTH)
            row_max = stream.tile([P, POOL_BLOCKS * CHUNK // (2 * WIDTH), WIDTH], F32, name="row_max")
            nc.vector.tensor_max(out=row_max[:], in0=row_pairs[:, :, 0, :], in1=row_pairs[:, :, 1, :])
            column_pairs = row_max[:].rearrange("p (b a) (x d) -> p b (a x) d", b=POOL_BLOCKS, d=2)
            pooled = stream.tile([P, POOL_BLOCKS, POOLED], F32, name="pooled", bufs=3)
            nc.vector.tensor_max(
                out=pooled[:], in0=column_pairs[:, :, :, 0], in1=column_pairs[:, :, :, 1]
            )
            nc.sync.dma_start(
                out=out_1[0, :, c * POOLED : (c + 1) * POOLED], in_=pooled[:, V_BLOCKS, :]
            )

            v_bank = psum.tile([P, CHUNK], F32, name="bank")
            for b in range(V_BLOCKS):
                nc.tensor.transpose(v_bank[:, b * P : (b + 1) * P], pooled[:, b, :], identity[:])
            v_rows = resident.tile([P, CHUNK], F32, name="v_rows")
            nc.scalar.copy(out=v_rows[:], in_=v_bank[:])
            nc.sync.dma_start(out=out_2[0, c * POOLED : (c + 1) * POOLED, :], in_=v_rows[:])

        quantised = [quantise_chunk(0)]
        transpose_weights(0)
        transpose_weights(1)
        quantise_weights(0, 2)
        widen_vectors()
        transpose_weights(2)
        transpose_weights(3)
        transpose_weights(K_BLOCK)
        turn_vectors()
        quantise_weights(2, 2)
        transpose_weights(Q_BLOCK)
        fold_batch_norms()
        quantise_weights(K_BLOCK, 2)
        results = []
        for c in range(CHUNKS + 2):
            if c < CHUNKS:
                if c > 0:
                    quantised.append(quantise_chunk(c))
                results.append(convolve_chunk(*quantised[c]))
                finish_q(c, results[c][0])
            if c >= 2:
                finish_kv(c - 2, results[c - 2][1])
